import numpy as np
import ml_dtypes

BF16 = ml_dtypes.bfloat16


def bf(x):
    return np.asarray(x, np.float32).astype(BF16)


def f32(x):
    return np.asarray(x, np.float32)


def f64(x):
    return np.asarray(x).astype(np.float64)


def striped(idx):
    return np.tile(idx.reshape(-1, 16).T, (8, 1))


C, S, N, M = 512, 2048, 512, 1024


def setup_inputs():
    return {"cache": f32(np.random.standard_normal((C, S))), "gain": f32(1.0 + 0.1 * np.random.standard_normal((C, 1))), "w_up": bf(np.random.standard_normal((C, M)) / np.sqrt(C)), "offs": striped(np.random.permutation(S)[:N])}


def reference(cache, gain, w_up, offs):
    idx = offs[:16].T.reshape(-1)
    picked = f64(cache)[:, idx]
    n = f64(gain) * picked / np.sqrt(np.mean(picked * picked, axis=0, keepdims=True))
    return f64(w_up).T @ n

@@ -1,0 +1,76 @@
+import concourse.mybir as mybir
+
+F32 = mybir.dt.float32
+BF16 = mybir.dt.bfloat16
+U16 = mybir.dt.uint16
+MULT = mybir.AluOpType.mult
+COPY = mybir.ActivationFunctionType.Copy
+RSQRT = mybir.ActivationFunctionType.Abs_reciprocal_sqrt
+
+P = 128
+C, S, N, M = 512, 2048, 512, 1024
+CB = C // P
+MB = M // P
+
+FLOPS = 2 * C * M * N
+
+
+def tile_mla_kernel(tc, cache, gain, w_up, offs, out):
+    nc = tc.nc
+    with (
+        tc.tile_pool(name="held", bufs=1) as held,
+        tc.tile_pool(name="work", bufs=2) as work,
+        tc.tile_pool(name="staged", bufs=4) as staged,
+        tc.psum_pool(name="stat_psum", bufs=1) as stat_psum,
+        tc.psum_pool(name="acc_psum", bufs=4) as acc_psum,
+    ):
+        offsets = held.tile([P, N // 16], U16, name="offsets")
+        nc.sync.dma_start(offsets[:], offs)
+        windows = []
+        for c in range(CB):
+            window = held.tile([P, S], F32, name=f"window{c}")
+            nc.sync.dma_start(window[:], cache[c * P : (c + 1) * P, :])
+            windows.append(window)
+        weights = []
+        for c in range(CB):
+            weight = held.tile([P, M], BF16, name=f"weight{c}")
+            nc.sync.dma_start(weight[:], w_up[c * P : (c + 1) * P, :])
+            weights.append(weight)
+        gains = held.tile([P, CB], F32, name="gains")
+        with nc.allow_non_contiguous_dma(reason="512 single floats, one for each partition and block"):
+            nc.gpsimd.dma_start(gains[:], gain.rearrange("(c p) o -> p (c o)", p=P))
+
+        ones = held.tile([P, P], F32, name="ones")
+        nc.vector.memset(ones[:], 1.0)
+
+        sums = stat_psum.tile([P, N], F32, name="sums")
+        picked = []
+        for c in range(CB):
+            columns = held.tile([P, N], F32, name=f"picked{c}")
+            nc.scalar.activation(columns[:], windows[c][:].indirect(offsets[:]), COPY)
+            picked.append(columns)
+            squares = work.tile([P, N], F32, name="squares")
+            nc.vector.tensor_tensor(squares[:], columns[:], columns[:], MULT)
+            nc.tensor.matmul(sums[:], ones[:], squares[:], start=(c == 0), stop=(c == CB - 1))
+
+        rstd = held.tile([P, N], F32, name="rstd")
+        nc.scalar.activation(rstd[:], sums[:], RSQRT, scale=1.0 / C)
+
+        normed = []
+        for c in range(CB):
+            latent = held.tile([P, N], BF16, name=f"normed{c}")
+            nc.vector.scalar_tensor_tensor(latent[:], picked[c][:], gains[:, c : c + 1], rstd[:], MULT, MULT)
+            normed.append(latent)
+
+        for m in range(MB):
+            acc = acc_psum.tile([P, N], F32, name="acc")
+            for c in range(CB):
+                nc.tensor.matmul(
+                    acc[:], weights[c][:, m * P : (m + 1) * P], normed[c][:], start=(c == 0), stop=(c == CB - 1)
+                )
+            result = staged.tile([P, N], F32, name="result")
+            if m % 2 == 0:
+                nc.scalar.copy(result[:], acc[:])
+            else:
+                nc.vector.tensor_copy(result[:], acc[:])
+            nc.sync.dma_start(out[m * P : (m + 1) * P, :], result[:])

@@ -38,10 +38,13 @@ def tile_mla_kernel(tc, cache, gain, w_up, offs, out):
             weights.append(weight)
         gains = held.tile([P, CB], F32, name="gains")
         with nc.allow_non_contiguous_dma(reason="512 single floats, one for each partition and block"):
-            nc.gpsimd.dma_start(gains[:], gain.rearrange("(c p) o -> p (c o)", p=P))
+            nc.scalar.dma_start(gains[:], gain.rearrange("(c p) o -> p (c o)", p=P))
 
         ones = held.tile([P, P], F32, name="ones")
         nc.vector.memset(ones[:], 1.0)
+
+        warm = held.tile([P, 1], F32, name="warm")
+        nc.scalar.activation(warm[:], ones[:, 0:1], RSQRT)
 
         sums = stat_psum.tile([P, N], F32, name="sums")
         picked = []

@@ -11,6 +11,9 @@ P = 128
 C, S, N, M = 512, 2048, 512, 1024
 CB = C // P
 MB = M // P
+H = 2
+NH = N // H
+MG = M // 2
 
 FLOPS = 2 * C * M * N
 
@@ -19,10 +22,10 @@ def tile_mla_kernel(tc, cache, gain, w_up, offs, out):
     nc = tc.nc
     with (
         tc.tile_pool(name="held", bufs=1) as held,
-        tc.tile_pool(name="work", bufs=2) as work,
-        tc.tile_pool(name="staged", bufs=4) as staged,
+        tc.tile_pool(name="work", bufs=4) as work,
+        tc.tile_pool(name="staged", bufs=6) as staged,
         tc.psum_pool(name="stat_psum", bufs=1) as stat_psum,
-        tc.psum_pool(name="acc_psum", bufs=4) as acc_psum,
+        tc.psum_pool(name="acc_psum", bufs=6) as acc_psum,
     ):
         offsets = held.tile([P, N // 16], U16, name="offsets")
         nc.sync.dma_start(offsets[:], offs)
@@ -32,9 +35,9 @@ def tile_mla_kernel(tc, cache, gain, w_up, offs, out):
             nc.sync.dma_start(window[:], cache[c * P : (c + 1) * P, :])
             windows.append(window)
         weights = []
-        for c in range(CB):
-            weight = held.tile([P, M], BF16, name=f"weight{c}")
-            nc.sync.dma_start(weight[:], w_up[c * P : (c + 1) * P, :])
+        for g in range(M // MG):
+            weight = held.tile([P, CB, MG], BF16, name=f"weights{g}")
+            nc.sync.dma_start(weight[:], w_up.rearrange("(c p) m -> p c m", p=P)[:, :, g * MG : (g + 1) * MG])
             weights.append(weight)
         gains = held.tile([P, CB], F32, name="gains")
         with nc.allow_non_contiguous_dma(reason="512 single floats, one for each partition and block"):
@@ -46,34 +49,44 @@ def tile_mla_kernel(tc, cache, gain, w_up, offs, out):
         warm = held.tile([P, 1], F32, name="warm")
         nc.scalar.activation(warm[:], ones[:, 0:1], RSQRT)
 
-        sums = stat_psum.tile([P, N], F32, name="sums")
+        sums = [stat_psum.tile([P, NH], F32, name=f"sums{h}") for h in range(H)]
         picked = []
         for c in range(CB):
             columns = held.tile([P, N], F32, name=f"picked{c}")
-            nc.scalar.activation(columns[:], windows[c][:].indirect(offsets[:]), COPY)
             picked.append(columns)
-            squares = work.tile([P, N], F32, name="squares")
-            nc.vector.tensor_tensor(squares[:], columns[:], columns[:], MULT)
-            nc.tensor.matmul(sums[:], ones[:], squares[:], start=(c == 0), stop=(c == CB - 1))
-
-        rstd = held.tile([P, N], F32, name="rstd")
-        nc.scalar.activation(rstd[:], sums[:], RSQRT, scale=1.0 / C)
+            for h in range(H):
+                half = slice(h * NH, (h + 1) * NH)
+                piece = offsets[:, h * (NH // 16) : (h + 1) * (NH // 16)]
+                nc.scalar.activation(columns[:, half], windows[c][:].indirect(piece), COPY)
+                squares = work.tile([P, NH], F32, name="squares")
+                nc.vector.tensor_tensor(squares[:], columns[:, half], columns[:, half], MULT)
+                nc.tensor.matmul(sums[h][:], ones[:], squares[:], start=(c == 0), stop=(c == CB - 1))
 
         normed = []
-        for c in range(CB):
-            latent = held.tile([P, N], BF16, name=f"normed{c}")
-            nc.vector.scalar_tensor_tensor(latent[:], picked[c][:], gains[:, c : c + 1], rstd[:], MULT, MULT)
-            normed.append(latent)
-
-        for m in range(MB):
-            acc = acc_psum.tile([P, N], F32, name="acc")
+        for h in range(H):
+            half = slice(h * NH, (h + 1) * NH)
+            rstd = held.tile([P, NH], F32, name=f"rstd{h}")
+            nc.scalar.activation(rstd[:], sums[h][:], RSQRT, scale=1.0 / C)
+            latents = held.tile([P, CB, NH], BF16, name=f"normed{h}")
             for c in range(CB):
-                nc.tensor.matmul(
-                    acc[:], weights[c][:, m * P : (m + 1) * P], normed[c][:], start=(c == 0), stop=(c == CB - 1)
+                nc.vector.scalar_tensor_tensor(
+                    latents[:, c, :], picked[c][:, half], gains[:, c : c + 1], rstd[:], MULT, MULT
                 )
-            result = staged.tile([P, N], F32, name="result")
-            if m % 2 == 0:
-                nc.scalar.copy(result[:], acc[:])
-            else:
-                nc.vector.tensor_copy(result[:], acc[:])
-            nc.sync.dma_start(out[m * P : (m + 1) * P, :], result[:])
+            normed.append(latents)
+
+        for h in range(H):
+            half = slice(h * NH, (h + 1) * NH)
+            for m in range(MB):
+                weight = weights[m * P // MG]
+                first = m * P % MG
+                acc = acc_psum.tile([P, NH], F32, name="acc")
+                for c in range(CB):
+                    nc.tensor.matmul(
+                        acc[:], weight[:, c, first : first + P], normed[h][:, c, :], start=(c == 0), stop=(c == CB - 1)
+                    )
+                result = staged.tile([P, NH], F32, name="result")
+                if m % 2 == 0:
+                    nc.scalar.copy(result[:], acc[:])
+                else:
+                    nc.vector.tensor_copy(result[:], acc[:])
+                nc.sync.dma_start(out[m * P : (m + 1) * P, half], result[:])

@@ -14,6 +14,7 @@ MB = M // P
 H = 2
 NH = N // H
 MG = M // 2
+PAIR = 2
 
 FLOPS = 2 * C * M * N
 
@@ -34,14 +35,14 @@ def tile_mla_kernel(tc, cache, gain, w_up, offs, out):
             window = held.tile([P, S], F32, name=f"window{c}")
             nc.sync.dma_start(window[:], cache[c * P : (c + 1) * P, :])
             windows.append(window)
+        gains = held.tile([P, CB], F32, name="gains")
+        with nc.allow_non_contiguous_dma(reason="512 single floats, one for each partition and block"):
+            nc.sync.dma_start(gains[:], gain.rearrange("(c p) o -> p (c o)", p=P))
         weights = []
         for g in range(M // MG):
             weight = held.tile([P, CB, MG], BF16, name=f"weights{g}")
             nc.sync.dma_start(weight[:], w_up.rearrange("(c p) m -> p c m", p=P)[:, :, g * MG : (g + 1) * MG])
             weights.append(weight)
-        gains = held.tile([P, CB], F32, name="gains")
-        with nc.allow_non_contiguous_dma(reason="512 single floats, one for each partition and block"):
-            nc.scalar.dma_start(gains[:], gain.rearrange("(c p) o -> p (c o)", p=P))
 
         ones = held.tile([P, P], F32, name="ones")
         nc.vector.memset(ones[:], 1.0)
@@ -50,43 +51,42 @@ def tile_mla_kernel(tc, cache, gain, w_up, offs, out):
         nc.scalar.activation(warm[:], ones[:, 0:1], RSQRT)
 
         sums = [stat_psum.tile([P, NH], F32, name=f"sums{h}") for h in range(H)]
-        picked = []
+        picked = [[held.tile([P, NH], F32, name=f"picked{c}_{h}") for h in range(H)] for c in range(CB)]
         for c in range(CB):
-            columns = held.tile([P, N], F32, name=f"picked{c}")
-            picked.append(columns)
             for h in range(H):
-                half = slice(h * NH, (h + 1) * NH)
                 piece = offsets[:, h * (NH // 16) : (h + 1) * (NH // 16)]
-                nc.scalar.activation(columns[:, half], windows[c][:].indirect(piece), COPY)
+                nc.scalar.activation(picked[c][h][:], windows[c][:].indirect(piece), COPY)
                 squares = work.tile([P, NH], F32, name="squares")
-                nc.vector.tensor_tensor(squares[:], columns[:, half], columns[:, half], MULT)
+                nc.vector.tensor_tensor(squares[:], picked[c][h][:], picked[c][h][:], MULT)
                 nc.tensor.matmul(sums[h][:], ones[:], squares[:], start=(c == 0), stop=(c == CB - 1))
 
-        normed = []
+        normed = [[held.tile([P, NH], BF16, name=f"normed{c}_{h}") for h in range(H)] for c in range(CB)]
         for h in range(H):
-            half = slice(h * NH, (h + 1) * NH)
             rstd = held.tile([P, NH], F32, name=f"rstd{h}")
             nc.scalar.activation(rstd[:], sums[h][:], RSQRT, scale=1.0 / C)
-            latents = held.tile([P, CB, NH], BF16, name=f"normed{h}")
             for c in range(CB):
                 nc.vector.scalar_tensor_tensor(
-                    latents[:, c, :], picked[c][:, half], gains[:, c : c + 1], rstd[:], MULT, MULT
+                    normed[c][h][:], picked[c][h][:], gains[:, c : c + 1], rstd[:], MULT, MULT
                 )
-            normed.append(latents)
 
         for h in range(H):
             half = slice(h * NH, (h + 1) * NH)
-            for m in range(MB):
-                weight = weights[m * P // MG]
-                first = m * P % MG
-                acc = acc_psum.tile([P, NH], F32, name="acc")
+            for m0 in range(0, MB, PAIR):
+                accs = [acc_psum.tile([P, NH], F32, name="acc") for m in range(m0, m0 + PAIR)]
                 for c in range(CB):
-                    nc.tensor.matmul(
-                        acc[:], weight[:, c, first : first + P], normed[h][:, c, :], start=(c == 0), stop=(c == CB - 1)
-                    )
-                result = staged.tile([P, NH], F32, name="result")
-                if m % 2 == 0:
-                    nc.scalar.copy(result[:], acc[:])
-                else:
-                    nc.vector.tensor_copy(result[:], acc[:])
-                nc.sync.dma_start(out[m * P : (m + 1) * P, half], result[:])
+                    for m in range(m0, m0 + PAIR):
+                        first = m * P % MG
+                        nc.tensor.matmul(
+                            accs[m - m0][:],
+                            weights[m * P // MG][:, c, first : first + P],
+                            normed[c][h][:],
+                            start=(c == 0),
+                            stop=(c == CB - 1),
+                        )
+                for m in range(m0, m0 + PAIR):
+                    result = staged.tile([P, NH], F32, name="result")
+                    if m % 2 == 0:
+                        nc.scalar.copy(result[:], accs[m - m0][:])
+                    else:
+                        nc.vector.tensor_copy(result[:], accs[m - m0][:])
+                    nc.sync.dma_start(out[m * P : (m + 1) * P, half], result[:])

@@ -26,7 +26,7 @@ def tile_mla_kernel(tc, cache, gain, w_up, offs, out):
         tc.tile_pool(name="work", bufs=4) as work,
         tc.tile_pool(name="staged", bufs=6) as staged,
         tc.psum_pool(name="stat_psum", bufs=1) as stat_psum,
-        tc.psum_pool(name="acc_psum", bufs=6) as acc_psum,
+        tc.psum_pool(name="acc_psum", bufs=5) as acc_psum,
     ):
         offsets = held.tile([P, N // 16], U16, name="offsets")
         nc.sync.dma_start(offsets[:], offs)
@@ -35,17 +35,25 @@ def tile_mla_kernel(tc, cache, gain, w_up, offs, out):
             window = held.tile([P, S], F32, name=f"window{c}")
             nc.sync.dma_start(window[:], cache[c * P : (c + 1) * P, :])
             windows.append(window)
-        gains = held.tile([P, CB], F32, name="gains")
-        with nc.allow_non_contiguous_dma(reason="512 single floats, one for each partition and block"):
-            nc.sync.dma_start(gains[:], gain.rearrange("(c p) o -> p (c o)", p=P))
         weights = []
         for g in range(M // MG):
             weight = held.tile([P, CB, MG], BF16, name=f"weights{g}")
             nc.sync.dma_start(weight[:], w_up.rearrange("(c p) m -> p c m", p=P)[:, :, g * MG : (g + 1) * MG])
             weights.append(weight)
 
+        gain_row = held.tile([1, C], F32, name="gain_row")
+        nc.scalar.dma_start(gain_row[:], gain.rearrange("c o -> o c"))
+
         ones = held.tile([P, P], F32, name="ones")
         nc.vector.memset(ones[:], 1.0)
+
+        gains_psum = stat_psum.tile([P, CB], F32, name="gains_psum")
+        for c in range(CB):
+            nc.tensor.matmul(
+                gains_psum[:, c : c + 1], gain_row[:, c * P : (c + 1) * P], ones[0:1, 0:1], start=True, stop=True
+            )
+        gains = held.tile([P, CB], F32, name="gains")
+        nc.vector.tensor_copy(gains[:], gains_psum[:])
 
         warm = held.tile([P, 1], F32, name="warm")
         nc.scalar.activation(warm[:], ones[:, 0:1], RSQRT)

@@ -14,7 +14,6 @@ MB = M // P
 H = 2
 NH = N // H
 MG = M // 2
-PAIR = 2
 
 FLOPS = 2 * C * M * N
 
@@ -79,22 +78,20 @@ def tile_mla_kernel(tc, cache, gain, w_up, offs, out):
 
         for h in range(H):
             half = slice(h * NH, (h + 1) * NH)
-            for m0 in range(0, MB, PAIR):
-                accs = [acc_psum.tile([P, NH], F32, name="acc") for m in range(m0, m0 + PAIR)]
+            for m in range(MB):
+                first = m * P % MG
+                acc = acc_psum.tile([P, NH], F32, name="acc")
                 for c in range(CB):
-                    for m in range(m0, m0 + PAIR):
-                        first = m * P % MG
-                        nc.tensor.matmul(
-                            accs[m - m0][:],
-                            weights[m * P // MG][:, c, first : first + P],
-                            normed[c][h][:],
-                            start=(c == 0),
-                            stop=(c == CB - 1),
-                        )
-                for m in range(m0, m0 + PAIR):
-                    result = staged.tile([P, NH], F32, name="result")
-                    if m % 2 == 0:
-                        nc.scalar.copy(result[:], accs[m - m0][:])
-                    else:
-                        nc.vector.tensor_copy(result[:], accs[m - m0][:])
-                    nc.sync.dma_start(out[m * P : (m + 1) * P, half], result[:])
+                    nc.tensor.matmul(
+                        acc[:],
+                        weights[m * P // MG][:, c, first : first + P],
+                        normed[c][h][:],
+                        start=(c == 0),
+                        stop=(c == CB - 1),
+                    )
+                result = staged.tile([P, NH], F32, name="result")
+                if m % 2 == 0:
+                    nc.scalar.copy(result[:], acc[:])
+                else:
+                    nc.vector.tensor_copy(result[:], acc[:])
+                nc.sync.dma_start(out[m * P : (m + 1) * P, half], result[:])

@@ -4,6 +4,7 @@ F32 = mybir.dt.float32
 BF16 = mybir.dt.bfloat16
 U16 = mybir.dt.uint16
 MULT = mybir.AluOpType.mult
+ADD = mybir.AluOpType.add
 COPY = mybir.ActivationFunctionType.Copy
 RSQRT = mybir.ActivationFunctionType.Abs_reciprocal_sqrt
 
@@ -11,9 +12,10 @@ P = 128
 C, S, N, M = 512, 2048, 512, 1024
 CB = C // P
 MB = M // P
-H = 2
-NH = N // H
-MG = M // 2
+EARLY = MB - 1
+LATE = 2
+Q = 4
+NQ = N // Q
 
 FLOPS = 2 * C * M * N
 
@@ -22,76 +24,78 @@ def tile_mla_kernel(tc, cache, gain, w_up, offs, out):
     nc = tc.nc
     with (
         tc.tile_pool(name="held", bufs=1) as held,
-        tc.tile_pool(name="work", bufs=4) as work,
-        tc.tile_pool(name="staged", bufs=6) as staged,
-        tc.psum_pool(name="stat_psum", bufs=1) as stat_psum,
-        tc.psum_pool(name="acc_psum", bufs=5) as acc_psum,
+        tc.tile_pool(name="work", bufs=2) as work,
+        tc.tile_pool(name="staged", bufs=MB) as staged,
+        tc.psum_pool(name="psum", bufs=1) as psum,
     ):
         offsets = held.tile([P, N // 16], U16, name="offsets")
         nc.sync.dma_start(offsets[:], offs)
-        windows = []
+        windows = [held.tile([P, S], F32, name=f"window{c}") for c in range(CB)]
+        weights = [held.tile([P, M], BF16, name=f"weights{c}") for c in range(CB)]
         for c in range(CB):
-            window = held.tile([P, S], F32, name=f"window{c}")
-            nc.sync.dma_start(window[:], cache[c * P : (c + 1) * P, :])
-            windows.append(window)
-        weights = []
-        for g in range(M // MG):
-            weight = held.tile([P, CB, MG], BF16, name=f"weights{g}")
-            nc.sync.dma_start(weight[:], w_up.rearrange("(c p) m -> p c m", p=P)[:, :, g * MG : (g + 1) * MG])
-            weights.append(weight)
+            nc.sync.dma_start(windows[c][:], cache[c * P : (c + 1) * P, :])
+            if c < CB - LATE:
+                nc.sync.dma_start(weights[c][:], w_up[c * P : (c + 1) * P, :])
+        for c in range(CB - LATE, CB):
+            nc.sync.dma_start(weights[c][:], w_up[c * P : (c + 1) * P, :])
 
-        gain_row = held.tile([1, C], F32, name="gain_row")
-        nc.scalar.dma_start(gain_row[:], gain.rearrange("c o -> o c"))
+        gains = held.tile([P, CB], F32, name="gains")
+        nc.scalar.dma_start(gains[:], gain.rearrange("(c p) o -> p (c o)", p=P))
 
         ones = held.tile([P, P], F32, name="ones")
         nc.vector.memset(ones[:], 1.0)
 
-        gains_psum = stat_psum.tile([P, CB], F32, name="gains_psum")
-        for c in range(CB):
-            nc.tensor.matmul(
-                gains_psum[:, c : c + 1], gain_row[:, c * P : (c + 1) * P], ones[0:1, 0:1], start=True, stop=True
-            )
-        gains = held.tile([P, CB], F32, name="gains")
-        nc.vector.tensor_copy(gains[:], gains_psum[:])
-
         warm = held.tile([P, 1], F32, name="warm")
         nc.scalar.activation(warm[:], ones[:, 0:1], RSQRT)
 
-        sums = [stat_psum.tile([P, NH], F32, name=f"sums{h}") for h in range(H)]
-        picked = [[held.tile([P, NH], F32, name=f"picked{c}_{h}") for h in range(H)] for c in range(CB)]
-        for c in range(CB):
-            for h in range(H):
-                piece = offsets[:, h * (NH // 16) : (h + 1) * (NH // 16)]
-                nc.scalar.activation(picked[c][h][:], windows[c][:].indirect(piece), COPY)
-                squares = work.tile([P, NH], F32, name="squares")
-                nc.vector.tensor_tensor(squares[:], picked[c][h][:], picked[c][h][:], MULT)
-                nc.tensor.matmul(sums[h][:], ones[:], squares[:], start=(c == 0), stop=(c == CB - 1))
+        sums = psum.tile([P, N], F32, name="sums")
+        accs = [psum.tile([P, N], F32, name=f"acc{m}") for m in range(EARLY)]
+        scaled = [held.tile([P, N], BF16, name=f"scaled{c}") for c in range(CB)]
 
-        normed = [[held.tile([P, NH], BF16, name=f"normed{c}_{h}") for h in range(H)] for c in range(CB)]
-        for h in range(H):
-            rstd = held.tile([P, NH], F32, name=f"rstd{h}")
-            nc.scalar.activation(rstd[:], sums[h][:], RSQRT, scale=1.0 / C)
-            for c in range(CB):
-                nc.vector.scalar_tensor_tensor(
-                    normed[c][h][:], picked[c][h][:], gains[:, c : c + 1], rstd[:], MULT, MULT
-                )
+        def add_product(m, c):
+            nc.tensor.matmul(
+                accs[m][:],
+                weights[c][:, m * P : (m + 1) * P],
+                scaled[c][:],
+                start=(c == 0),
+                stop=(c == CB - 1),
+            )
 
-        for h in range(H):
-            half = slice(h * NH, (h + 1) * NH)
-            for m in range(MB):
-                first = m * P % MG
-                acc = acc_psum.tile([P, NH], F32, name="acc")
-                for c in range(CB):
-                    nc.tensor.matmul(
-                        acc[:],
-                        weights[m * P // MG][:, c, first : first + P],
-                        normed[c][h][:],
-                        start=(c == 0),
-                        stop=(c == CB - 1),
-                    )
-                result = staged.tile([P, NH], F32, name="result")
-                if m % 2 == 0:
-                    nc.scalar.copy(result[:], acc[:])
-                else:
-                    nc.vector.tensor_copy(result[:], acc[:])
-                nc.sync.dma_start(out[m * P : (m + 1) * P, half], result[:])
+        early_squares = held.tile([P, N], F32, name="early_squares")
+        for c in range(CB - 1):
+            picked = work.tile([P, N], F32, name="picked")
+            nc.scalar.activation(picked[:], windows[c][:].indirect(offsets[:]), COPY)
+            nc.vector.tensor_scalar_mul(scaled[c][:], picked[:], gains[:, c : c + 1])
+            if c == 0:
+                nc.vector.tensor_tensor(early_squares[:], picked[:], picked[:], MULT)
+            else:
+                squares = work.tile([P, N], F32, name="squares")
+                nc.vector.tensor_tensor(squares[:], picked[:], picked[:], MULT)
+                nc.vector.tensor_tensor(early_squares[:], early_squares[:], squares[:], ADD)
+            if c < CB - LATE:
+                for m in range(EARLY):
+                    add_product(m, c)
+        nc.tensor.matmul(sums[:], ones[:], early_squares[:], start=True, stop=False)
+
+        c = CB - 1
+        picked = work.tile([P, N], F32, name="picked")
+        squares = work.tile([P, N], F32, name="squares")
+        for q in range(Q):
+            cols = slice(q * NQ, (q + 1) * NQ)
+            piece = offsets[:, q * (NQ // 16) : (q + 1) * (NQ // 16)]
+            nc.scalar.activation(picked[:, cols], windows[c][:].indirect(piece), COPY)
+            nc.vector.tensor_tensor(squares[:, cols], picked[:, cols], picked[:, cols], MULT)
+            nc.tensor.matmul(sums[:, cols], ones[:], squares[:, cols], start=False, stop=(q == Q - 1))
+        nc.vector.tensor_scalar_mul(scaled[c][:], picked[:], gains[:, c : c + 1])
+
+        rstd = held.tile([P, N], F32, name="rstd")
+        nc.scalar.activation(rstd[:], sums[:], RSQRT, scale=1.0 / C)
+
+        accs.append(psum.tile([P, N], F32, name="last", tag="sums"))
+
+        for m in range(MB):
+            for c in range(CB - LATE if m < EARLY else 0, CB):
+                add_product(m, c)
+            result = staged.tile([P, N], F32, name="result")
+            nc.vector.tensor_tensor(result[:], accs[m][:], rstd[:], MULT)
+            nc.sync.dma_start(out[m * P : (m + 1) * P, :], result[:])

@@ -24,7 +24,6 @@ def tile_mla_kernel(tc, cache, gain, w_up, offs, out):
     nc = tc.nc
     with (
         tc.tile_pool(name="held", bufs=1) as held,
-        tc.tile_pool(name="work", bufs=2) as work,
         tc.tile_pool(name="staged", bufs=MB) as staged,
         tc.psum_pool(name="psum", bufs=1) as psum,
     ):
@@ -61,32 +60,29 @@ def tile_mla_kernel(tc, cache, gain, w_up, offs, out):
                 stop=(c == CB - 1),
             )
 
-        early_squares = held.tile([P, N], F32, name="early_squares")
-        for c in range(CB - 1):
-            picked = work.tile([P, N], F32, name="picked")
-            nc.scalar.activation(picked[:], windows[c][:].indirect(offsets[:]), COPY)
-            nc.vector.tensor_scalar_mul(scaled[c][:], picked[:], gains[:, c : c + 1])
-            if c == 0:
-                nc.vector.tensor_tensor(early_squares[:], picked[:], picked[:], MULT)
-            else:
-                squares = work.tile([P, N], F32, name="squares")
-                nc.vector.tensor_tensor(squares[:], picked[:], picked[:], MULT)
-                nc.vector.tensor_tensor(early_squares[:], early_squares[:], squares[:], ADD)
-            if c < CB - LATE:
-                for m in range(EARLY):
-                    add_product(m, c)
-        nc.tensor.matmul(sums[:], ones[:], early_squares[:], start=True, stop=False)
+        picked = [held.tile([P, N], F32, name=f"picked{c}") for c in range(CB)]
+        squares = [held.tile([P, N], F32, name=f"squares{c}") for c in range(CB)]
 
-        c = CB - 1
-        picked = work.tile([P, N], F32, name="picked")
-        squares = work.tile([P, N], F32, name="squares")
-        for q in range(Q):
-            cols = slice(q * NQ, (q + 1) * NQ)
-            piece = offsets[:, q * (NQ // 16) : (q + 1) * (NQ // 16)]
-            nc.scalar.activation(picked[:, cols], windows[c][:].indirect(piece), COPY)
-            nc.vector.tensor_tensor(squares[:, cols], picked[:, cols], picked[:, cols], MULT)
-            nc.tensor.matmul(sums[:, cols], ones[:], squares[:, cols], start=False, stop=(q == Q - 1))
-        nc.vector.tensor_scalar_mul(scaled[c][:], picked[:], gains[:, c : c + 1])
+        for c in range(CB - LATE):
+            nc.scalar.activation(picked[c][:], windows[c][:].indirect(offsets[:]), COPY)
+            nc.vector.tensor_scalar_mul(scaled[c][:], picked[c][:], gains[:, c : c + 1])
+            nc.vector.tensor_tensor(squares[c][:], picked[c][:], picked[c][:], MULT)
+            if c > 0:
+                nc.vector.tensor_tensor(squares[0][:], squares[0][:], squares[c][:], ADD)
+            for m in range(EARLY):
+                add_product(m, c)
+        nc.tensor.matmul(sums[:], ones[:], squares[0][:], start=True, stop=False)
+
+        for c in range(CB - LATE, CB):
+            for q in range(Q):
+                cols = slice(q * NQ, (q + 1) * NQ)
+                piece = offsets[:, q * (NQ // 16) : (q + 1) * (NQ // 16)]
+                nc.scalar.activation(picked[c][:, cols], windows[c][:].indirect(piece), COPY)
+                nc.vector.tensor_tensor(squares[c][:, cols], picked[c][:, cols], picked[c][:, cols], MULT)
+                nc.tensor.matmul(
+                    sums[:, cols], ones[:], squares[c][:, cols], start=False, stop=(c == CB - 1 and q == Q - 1)
+                )
+            nc.vector.tensor_scalar_mul(scaled[c][:], picked[c][:], gains[:, c : c + 1])
 
         rstd = held.tile([P, N], F32, name="rstd")
         nc.scalar.activation(rstd[:], sums[:], RSQRT, scale=1.0 / C)

@@ -5,6 +5,7 @@ BF16 = mybir.dt.bfloat16
 U16 = mybir.dt.uint16
 MULT = mybir.AluOpType.mult
 ADD = mybir.AluOpType.add
+SUBTRACT = mybir.AluOpType.subtract
 COPY = mybir.ActivationFunctionType.Copy
 RSQRT = mybir.ActivationFunctionType.Abs_reciprocal_sqrt
 
@@ -43,6 +44,8 @@ def tile_mla_kernel(tc, cache, gain, w_up, offs, out):
 
         ones = held.tile([P, P], F32, name="ones")
         nc.vector.memset(ones[:], 1.0)
+        ones_bf16 = held.tile([P, P], BF16, name="ones_bf16")
+        nc.vector.memset(ones_bf16[:], 1.0)
 
         warm = held.tile([P, 1], F32, name="warm")
         nc.scalar.activation(warm[:], ones[:, 0:1], RSQRT)
@@ -71,7 +74,12 @@ def tile_mla_kernel(tc, cache, gain, w_up, offs, out):
                 nc.vector.tensor_tensor(squares[0][:], squares[0][:], squares[c][:], ADD)
             for m in range(EARLY):
                 add_product(m, c)
-        nc.tensor.matmul(sums[:], ones[:], squares[0][:], start=True, stop=False)
+        rounded = held.tile([P, N], BF16, name="rounded")
+        nc.vector.tensor_copy(rounded[:], squares[0][:])
+        left_over = held.tile([P, N], BF16, name="left_over")
+        nc.vector.tensor_tensor(left_over[:], squares[0][:], rounded[:], SUBTRACT)
+        nc.tensor.matmul(sums[:], ones_bf16[:], rounded[:], start=True, stop=False)
+        nc.tensor.matmul(sums[:], ones_bf16[:], left_over[:], start=False, stop=False)
 
         for c in range(CB - LATE, CB):
             for q in range(Q):

@@ -101,5 +101,8 @@ def tile_mla_kernel(tc, cache, gain, w_up, offs, out):
             for c in range(CB - LATE if m < EARLY else 0, CB):
                 add_product(m, c)
             result = staged.tile([P, N], F32, name="result")
-            nc.vector.tensor_tensor(result[:], accs[m][:], rstd[:], MULT)
-            nc.sync.dma_start(out[m * P : (m + 1) * P, :], result[:])
+            pieces = Q if m == MB - 1 else 1
+            for q in range(pieces):
+                cols = slice(q * (N // pieces), (q + 1) * (N // pieces))
+                nc.vector.tensor_tensor(result[:, cols], accs[m][:, cols], rstd[:, cols], MULT)
+                nc.sync.dma_start(out[m * P : (m + 1) * P, cols], result[:, cols])

@@ -51,6 +51,11 @@ def tile_mla_kernel(tc, cache, gain, w_up, offs, out):
         nc.scalar.activation(warm[:], ones[:, 0:1], RSQRT)
 
         sums = psum.tile([P, N], F32, name="sums")
+
+        zeros = held.tile([P, N], BF16, name="zeros")
+        nc.vector.memset(zeros[:], 0.0)
+        for w in range(2 * 4096 // N):
+            nc.tensor.matmul(sums[:], ones_bf16[:], zeros[:], start=True, stop=True)
         accs = [psum.tile([P, N], F32, name=f"acc{m}") for m in range(EARLY)]
         scaled = [held.tile([P, N], BF16, name=f"scaled{c}") for c in range(CB)]
 

@@ -4,9 +4,9 @@ F32 = mybir.dt.float32
 BF16 = mybir.dt.bfloat16
 U16 = mybir.dt.uint16
 MULT = mybir.AluOpType.mult
-ADD = mybir.AluOpType.add
 SUBTRACT = mybir.AluOpType.subtract
 COPY = mybir.ActivationFunctionType.Copy
+SQUARE = mybir.ActivationFunctionType.Square
 RSQRT = mybir.ActivationFunctionType.Abs_reciprocal_sqrt
 
 P = 128
@@ -28,19 +28,23 @@ def tile_mla_kernel(tc, cache, gain, w_up, offs, out):
         tc.tile_pool(name="staged", bufs=MB) as staged,
         tc.psum_pool(name="psum", bufs=1) as psum,
     ):
+        cache_blocks = cache.rearrange("(p c) s -> p c s", p=P)
+        w_up_blocks = w_up.rearrange("(p c) m -> p c m", p=P)
+
         offsets = held.tile([P, N // 16], U16, name="offsets")
-        nc.sync.dma_start(offsets[:], offs)
         windows = [held.tile([P, S], F32, name=f"window{c}") for c in range(CB)]
         weights = [held.tile([P, M], BF16, name=f"weights{c}") for c in range(CB)]
         for c in range(CB):
-            nc.sync.dma_start(windows[c][:], cache[c * P : (c + 1) * P, :])
+            nc.sync.dma_start(windows[c][:], cache_blocks[:, c, :])
+            if c == 0:
+                nc.sync.dma_start(offsets[:], offs)
             if c < CB - LATE:
-                nc.sync.dma_start(weights[c][:], w_up[c * P : (c + 1) * P, :])
+                nc.sync.dma_start(weights[c][:], w_up_blocks[:, c, :])
         for c in range(CB - LATE, CB):
-            nc.sync.dma_start(weights[c][:], w_up[c * P : (c + 1) * P, :])
+            nc.sync.dma_start(weights[c][:], w_up_blocks[:, c, :])
 
         gains = held.tile([P, CB], F32, name="gains")
-        nc.scalar.dma_start(gains[:], gain.rearrange("(c p) o -> p (c o)", p=P))
+        nc.scalar.dma_start(gains[:], gain.rearrange("(p c) o -> p (c o)", p=P))
 
         ones = held.tile([P, P], F32, name="ones")
         nc.vector.memset(ones[:], 1.0)
@@ -71,20 +75,18 @@ def tile_mla_kernel(tc, cache, gain, w_up, offs, out):
         picked = [held.tile([P, N], F32, name=f"picked{c}") for c in range(CB)]
         squares = [held.tile([P, N], F32, name=f"squares{c}") for c in range(CB)]
 
+        rounded = [held.tile([P, N], BF16, name=f"rounded{c}") for c in range(CB - LATE)]
+        left_over = [held.tile([P, N], BF16, name=f"left_over{c}") for c in range(CB - LATE)]
         for c in range(CB - LATE):
             nc.scalar.activation(picked[c][:], windows[c][:].indirect(offsets[:]), COPY)
             nc.vector.tensor_scalar_mul(scaled[c][:], picked[c][:], gains[:, c : c + 1])
-            nc.vector.tensor_tensor(squares[c][:], picked[c][:], picked[c][:], MULT)
-            if c > 0:
-                nc.vector.tensor_tensor(squares[0][:], squares[0][:], squares[c][:], ADD)
+            nc.scalar.activation(squares[c][:], picked[c][:], SQUARE)
+            nc.vector.tensor_copy(rounded[c][:], squares[c][:])
+            nc.vector.tensor_tensor(left_over[c][:], squares[c][:], rounded[c][:], SUBTRACT)
             for m in range(EARLY):
                 add_product(m, c)
-        rounded = held.tile([P, N], BF16, name="rounded")
-        nc.vector.tensor_copy(rounded[:], squares[0][:])
-        left_over = held.tile([P, N], BF16, name="left_over")
-        nc.vector.tensor_tensor(left_over[:], squares[0][:], rounded[:], SUBTRACT)
-        nc.tensor.matmul(sums[:], ones_bf16[:], rounded[:], start=True, stop=False)
-        nc.tensor.matmul(sums[:], ones_bf16[:], left_over[:], start=False, stop=False)
+            nc.tensor.matmul(sums[:], ones_bf16[:], rounded[c][:], start=(c == 0), stop=False)
+            nc.tensor.matmul(sums[:], ones_bf16[:], left_over[c][:], start=False, stop=False)
 
         for c in range(CB - LATE, CB):
             for q in range(Q):
@@ -98,7 +100,9 @@ def tile_mla_kernel(tc, cache, gain, w_up, offs, out):
             nc.vector.tensor_scalar_mul(scaled[c][:], picked[c][:], gains[:, c : c + 1])
 
         rstd = held.tile([P, N], F32, name="rstd")
-        nc.scalar.activation(rstd[:], sums[:], RSQRT, scale=1.0 / C)
+        for h in range(2):
+            cols = slice(h * (N // 2), (h + 1) * (N // 2))
+            nc.scalar.activation(rstd[:, cols], sums[:, cols], RSQRT, scale=1.0 / C)
 
         accs.append(psum.tile([P, N], F32, name="last", tag="sums"))
 
@@ -106,7 +110,7 @@ def tile_mla_kernel(tc, cache, gain, w_up, offs, out):
             for c in range(CB - LATE if m < EARLY else 0, CB):
                 add_product(m, c)
             result = staged.tile([P, N], F32, name="result")
-            pieces = Q if m == MB - 1 else 1
+            pieces = {0: 2, MB - 1: Q}.get(m, 1)
             for q in range(pieces):
                 cols = slice(q * (N // pieces), (q + 1) * (N // pieces))
                 nc.vector.tensor_tensor(result[:, cols], accs[m][:, cols], rstd[:, cols], MULT)

@@ -15,6 +15,7 @@ CB = C // P
 MB = M // P
 EARLY = MB - 1
 LATE = 2
+EARLY_M = EARLY * P
 Q = 4
 NQ = N // Q
 
@@ -33,15 +34,17 @@ def tile_mla_kernel(tc, cache, gain, w_up, offs, out):
 
         offsets = held.tile([P, N // 16], U16, name="offsets")
         windows = [held.tile([P, S], F32, name=f"window{c}") for c in range(CB)]
-        weights = [held.tile([P, M], BF16, name=f"weights{c}") for c in range(CB)]
+        weights = [held.tile([P, EARLY_M], BF16, name=f"weights{c}") for c in range(CB)]
+        last_weights = held.tile([P, CB, P], BF16, name="last_weights")
         for c in range(CB):
             nc.sync.dma_start(windows[c][:], cache_blocks[:, c, :])
             if c == 0:
                 nc.sync.dma_start(offsets[:], offs)
             if c < CB - LATE:
-                nc.sync.dma_start(weights[c][:], w_up_blocks[:, c, :])
+                nc.sync.dma_start(weights[c][:], w_up_blocks[:, c, :EARLY_M])
         for c in range(CB - LATE, CB):
-            nc.sync.dma_start(weights[c][:], w_up_blocks[:, c, :])
+            nc.sync.dma_start(weights[c][:], w_up_blocks[:, c, :EARLY_M])
+        nc.sync.dma_start(last_weights[:], w_up_blocks[:, :, EARLY_M:])
 
         gains = held.tile([P, CB], F32, name="gains")
         nc.scalar.dma_start(gains[:], gain.rearrange("(p c) o -> p (c o)", p=P))
@@ -58,7 +61,7 @@ def tile_mla_kernel(tc, cache, gain, w_up, offs, out):
 
         zeros = held.tile([P, N], BF16, name="zeros")
         nc.vector.memset(zeros[:], 0.0)
-        for w in range(2 * 4096 // N):
+        for w in range(3 * 4096 // 2 // N):
             nc.tensor.matmul(sums[:], ones_bf16[:], zeros[:], start=True, stop=True)
         accs = [psum.tile([P, N], F32, name=f"acc{m}") for m in range(EARLY)]
         scaled = [held.tile([P, N], BF16, name=f"scaled{c}") for c in range(CB)]
@@ -66,7 +69,7 @@ def tile_mla_kernel(tc, cache, gain, w_up, offs, out):
         def add_product(m, c):
             nc.tensor.matmul(
                 accs[m][:],
-                weights[c][:, m * P : (m + 1) * P],
+                weights[c][:, m * P : (m + 1) * P] if m < EARLY else last_weights[:, c, :],
                 scaled[c][:],
                 start=(c == 0),
                 stop=(c == CB - 1),

@@ -13,11 +13,13 @@ P = 128
 C, S, N, M = 512, 2048, 512, 1024
 CB = C // P
 MB = M // P
-EARLY = MB - 1
+HALVES = 2
+EARLY = MB - HALVES
 LATE = 2
 EARLY_M = EARLY * P
 Q = 4
 NQ = N // Q
+NH = N // HALVES
 
 FLOPS = 2 * C * M * N
 
@@ -35,7 +37,7 @@ def tile_mla_kernel(tc, cache, gain, w_up, offs, out):
         offsets = held.tile([P, N // 16], U16, name="offsets")
         windows = [held.tile([P, S], F32, name=f"window{c}") for c in range(CB)]
         weights = [held.tile([P, EARLY_M], BF16, name=f"weights{c}") for c in range(CB)]
-        last_weights = held.tile([P, CB, P], BF16, name="last_weights")
+        last_weights = held.tile([P, CB, M - EARLY_M], BF16, name="last_weights")
         for c in range(CB):
             nc.sync.dma_start(windows[c][:], cache_blocks[:, c, :])
             if c == 0:
@@ -57,19 +59,23 @@ def tile_mla_kernel(tc, cache, gain, w_up, offs, out):
         warm = held.tile([P, 1], F32, name="warm")
         nc.scalar.activation(warm[:], ones[:, 0:1], RSQRT)
 
-        sums = psum.tile([P, N], F32, name="sums")
+        sums = [psum.tile([P, N], F32, name=f"sums{h}") for h in range(HALVES)]
 
         zeros = held.tile([P, N], BF16, name="zeros")
         nc.vector.memset(zeros[:], 0.0)
         for w in range(3 * 4096 // 2 // N):
-            nc.tensor.matmul(sums[:], ones_bf16[:], zeros[:], start=True, stop=True)
+            nc.tensor.matmul(sums[0][:], ones_bf16[:], zeros[:], start=True, stop=True)
         accs = [psum.tile([P, N], F32, name=f"acc{m}") for m in range(EARLY)]
         scaled = [held.tile([P, N], BF16, name=f"scaled{c}") for c in range(CB)]
 
         def add_product(m, c):
+            if m < EARLY:
+                block = weights[c][:, m * P : (m + 1) * P]
+            else:
+                block = last_weights[:, c, (m - EARLY) * P : (m - EARLY + 1) * P]
             nc.tensor.matmul(
                 accs[m][:],
-                weights[c][:, m * P : (m + 1) * P] if m < EARLY else last_weights[:, c, :],
+                block,
                 scaled[c][:],
                 start=(c == 0),
                 stop=(c == CB - 1),
@@ -88,8 +94,11 @@ def tile_mla_kernel(tc, cache, gain, w_up, offs, out):
             nc.vector.tensor_tensor(left_over[c][:], squares[c][:], rounded[c][:], SUBTRACT)
             for m in range(EARLY):
                 add_product(m, c)
-            nc.tensor.matmul(sums[:], ones_bf16[:], rounded[c][:], start=(c == 0), stop=False)
-            nc.tensor.matmul(sums[:], ones_bf16[:], left_over[c][:], start=False, stop=False)
+            for h in range(HALVES):
+                cols = slice(h * NH, (h + 1) * NH)
+                total = sums[h][:, cols]
+                nc.tensor.matmul(total, ones_bf16[:], rounded[c][:, cols], start=(c == 0), stop=False)
+                nc.tensor.matmul(total, ones_bf16[:], left_over[c][:, cols], start=False, stop=False)
 
         for c in range(CB - LATE, CB):
             for q in range(Q):
@@ -97,23 +106,27 @@ def tile_mla_kernel(tc, cache, gain, w_up, offs, out):
                 piece = offsets[:, q * (NQ // 16) : (q + 1) * (NQ // 16)]
                 nc.scalar.activation(picked[c][:, cols], windows[c][:].indirect(piece), COPY)
                 nc.vector.tensor_tensor(squares[c][:, cols], picked[c][:, cols], picked[c][:, cols], MULT)
+                h = cols.start // NH
                 nc.tensor.matmul(
-                    sums[:, cols], ones[:], squares[c][:, cols], start=False, stop=(c == CB - 1 and q == Q - 1)
+                    sums[h][:, cols],
+                    ones[:],
+                    squares[c][:, cols],
+                    start=False,
+                    stop=(c == CB - 1 and cols.stop == (h + 1) * NH),
                 )
             nc.vector.tensor_scalar_mul(scaled[c][:], picked[c][:], gains[:, c : c + 1])
 
         rstd = held.tile([P, N], F32, name="rstd")
-        for h in range(2):
-            cols = slice(h * (N // 2), (h + 1) * (N // 2))
-            nc.scalar.activation(rstd[:, cols], sums[:, cols], RSQRT, scale=1.0 / C)
-
-        accs.append(psum.tile([P, N], F32, name="last", tag="sums"))
+        for h in range(HALVES):
+            cols = slice(h * NH, (h + 1) * NH)
+            nc.scalar.activation(rstd[:, cols], sums[h][:, cols], RSQRT, scale=1.0 / C)
+            accs.append(psum.tile([P, N], F32, name=f"acc{EARLY + h}", tag=f"sums{h}"))
 
         for m in range(MB):
             for c in range(CB - LATE if m < EARLY else 0, CB):
                 add_product(m, c)
             result = staged.tile([P, N], F32, name="result")
-            pieces = {0: 2, MB - 1: Q}.get(m, 1)
+            pieces = HALVES if m == 0 else Q if m == MB - 1 else 1
             for q in range(pieces):
                 cols = slice(q * (N // pieces), (q + 1) * (N // pieces))
                 nc.vector.tensor_tensor(result[:, cols], accs[m][:, cols], rstd[:, cols], MULT)

@@ -20,6 +20,7 @@ EARLY_M = EARLY * P
 Q = 4
 NQ = N // Q
 NH = N // HALVES
+FILL = 3
 
 FLOPS = 2 * C * M * N
 
@@ -101,6 +102,9 @@ def tile_mla_kernel(tc, cache, gain, w_up, offs, out):
                 nc.tensor.matmul(total, ones_bf16[:], left_over[c][:, cols], start=False, stop=False)
 
         for c in range(CB - LATE, CB):
+            if c == CB - 1:
+                for m in range(FILL):
+                    add_product(m, c - 1)
             for q in range(Q):
                 cols = slice(q * NQ, (q + 1) * NQ)
                 piece = offsets[:, q * (NQ // 16) : (q + 1) * (NQ // 16)]
@@ -123,7 +127,8 @@ def tile_mla_kernel(tc, cache, gain, w_up, offs, out):
             accs.append(psum.tile([P, N], F32, name=f"acc{EARLY + h}", tag=f"sums{h}"))
 
         for m in range(MB):
-            for c in range(CB - LATE if m < EARLY else 0, CB):
+            first = 0 if m >= EARLY else CB - 1 if m < FILL else CB - LATE
+            for c in range(first, CB):
                 add_product(m, c)
             result = staged.tile([P, N], F32, name="result")
             pieces = HALVES if m == 0 else Q if m == MB - 1 else 1

@@ -69,15 +69,15 @@ def tile_mla_kernel(tc, cache, gain, w_up, offs, out):
         accs = [psum.tile([P, N], F32, name=f"acc{m}") for m in range(EARLY)]
         scaled = [held.tile([P, N], BF16, name=f"scaled{c}") for c in range(CB)]
 
-        def add_product(m, c):
+        def add_product(acc, m, c, cols=slice(0, N)):
             if m < EARLY:
                 block = weights[c][:, m * P : (m + 1) * P]
             else:
                 block = last_weights[:, c, (m - EARLY) * P : (m - EARLY + 1) * P]
             nc.tensor.matmul(
-                accs[m][:],
+                acc[:, cols],
                 block,
-                scaled[c][:],
+                scaled[c][:, cols],
                 start=(c == 0),
                 stop=(c == CB - 1),
             )
@@ -94,7 +94,7 @@ def tile_mla_kernel(tc, cache, gain, w_up, offs, out):
             nc.vector.tensor_copy(rounded[c][:], squares[c][:])
             nc.vector.tensor_tensor(left_over[c][:], squares[c][:], rounded[c][:], SUBTRACT)
             for m in range(EARLY):
-                add_product(m, c)
+                add_product(accs[m], m, c)
             for h in range(HALVES):
                 cols = slice(h * NH, (h + 1) * NH)
                 total = sums[h][:, cols]
@@ -104,7 +104,7 @@ def tile_mla_kernel(tc, cache, gain, w_up, offs, out):
         for c in range(CB - LATE, CB):
             if c == CB - 1:
                 for m in range(FILL):
-                    add_product(m, c - 1)
+                    add_product(accs[m], m, c - 1)
             for q in range(Q):
                 cols = slice(q * NQ, (q + 1) * NQ)
                 piece = offsets[:, q * (NQ // 16) : (q + 1) * (NQ // 16)]
@@ -128,11 +128,17 @@ def tile_mla_kernel(tc, cache, gain, w_up, offs, out):
 
         for m in range(MB):
             first = 0 if m >= EARLY else CB - 1 if m < FILL else CB - LATE
-            for c in range(first, CB):
-                add_product(m, c)
             result = staged.tile([P, N], F32, name="result")
-            pieces = HALVES if m == 0 else Q if m == MB - 1 else 1
-            for q in range(pieces):
-                cols = slice(q * (N // pieces), (q + 1) * (N // pieces))
-                nc.vector.tensor_tensor(result[:, cols], accs[m][:, cols], rstd[:, cols], MULT)
-                nc.sync.dma_start(out[m * P : (m + 1) * P, cols], result[:, cols])
+            if m < MB - 1:
+                parts = [(accs[m], slice(0, N))]
+            else:
+                spare = psum.tile([P, N], F32, name="spare", tag="acc0")
+                parts = [(accs[m], slice(0, NH)), (spare, slice(NH, N))]
+            width = NH if m == 0 else NQ if m == MB - 1 else N
+            for acc, part in parts:
+                for c in range(first, CB):
+                    add_product(acc, m, c, part)
+                for begin in range(part.start, part.stop, width):
+                    cols = slice(begin, begin + width)
+                    nc.vector.tensor_tensor(result[:, cols], acc[:, cols], rstd[:, cols], MULT)
+                    nc.sync.dma_start(out[m * P : (m + 1) * P, cols], result[:, cols])

@@ -14,7 +14,8 @@ C, S, N, M = 512, 2048, 512, 1024
 CB = C // P
 MB = M // P
 HALVES = 2
-EARLY = MB - HALVES
+BANKED = MB - HALVES
+EARLY = 5
 LATE = 2
 EARLY_M = EARLY * P
 Q = 4
@@ -66,7 +67,7 @@ def tile_mla_kernel(tc, cache, gain, w_up, offs, out):
         nc.vector.memset(zeros[:], 0.0)
         for w in range(3 * 4096 // 2 // N):
             nc.tensor.matmul(sums[0][:], ones_bf16[:], zeros[:], start=True, stop=True)
-        accs = [psum.tile([P, N], F32, name=f"acc{m}") for m in range(EARLY)]
+        accs = [psum.tile([P, N], F32, name=f"acc{m}") for m in range(BANKED)]
         scaled = [held.tile([P, N], BF16, name=f"scaled{c}") for c in range(CB)]
 
         def add_product(acc, m, c, cols=slice(0, N)):
@@ -124,7 +125,7 @@ def tile_mla_kernel(tc, cache, gain, w_up, offs, out):
         for h in range(HALVES):
             cols = slice(h * NH, (h + 1) * NH)
             nc.scalar.activation(rstd[:, cols], sums[h][:, cols], RSQRT, scale=1.0 / C)
-            accs.append(psum.tile([P, N], F32, name=f"acc{EARLY + h}", tag=f"sums{h}"))
+            accs.append(psum.tile([P, N], F32, name=f"acc{BANKED + h}", tag=f"sums{h}"))
 
         for m in range(MB):
             first = 0 if m >= EARLY else CB - 1 if m < FILL else CB - LATE
@@ -134,7 +135,7 @@ def tile_mla_kernel(tc, cache, gain, w_up, offs, out):
             else:
                 spare = psum.tile([P, N], F32, name="spare", tag="acc0")
                 parts = [(accs[m], slice(0, NH)), (spare, slice(NH, N))]
-            width = NH if m == 0 else NQ if m == MB - 1 else N
+            width = NH if m in (0, MB - 1) else N
             for acc, part in parts:
                 for c in range(first, CB):
                     add_product(acc, m, c, part)

@@ -14,8 +14,7 @@ C, S, N, M = 512, 2048, 512, 1024
 CB = C // P
 MB = M // P
 HALVES = 2
-BANKED = MB - HALVES
-EARLY = 5
+EARLY = MB - HALVES
 LATE = 2
 EARLY_M = EARLY * P
 Q = 4
@@ -30,7 +29,6 @@ def tile_mla_kernel(tc, cache, gain, w_up, offs, out):
     nc = tc.nc
     with (
         tc.tile_pool(name="held", bufs=1) as held,
-        tc.tile_pool(name="staged", bufs=MB) as staged,
         tc.psum_pool(name="psum", bufs=1) as psum,
     ):
         cache_blocks = cache.rearrange("(p c) s -> p c s", p=P)
@@ -67,21 +65,25 @@ def tile_mla_kernel(tc, cache, gain, w_up, offs, out):
         nc.vector.memset(zeros[:], 0.0)
         for w in range(3 * 4096 // 2 // N):
             nc.tensor.matmul(sums[0][:], ones_bf16[:], zeros[:], start=True, stop=True)
-        accs = [psum.tile([P, N], F32, name=f"acc{m}") for m in range(BANKED)]
+        accs = [psum.tile([P, N], F32, name=f"acc{m}") for m in range(EARLY)]
         scaled = [held.tile([P, N], BF16, name=f"scaled{c}") for c in range(CB)]
+        results = [held.tile([P, N], F32, name=f"result{m}") for m in range(MB)]
+        added = [0] * MB
 
-        def add_product(acc, m, c, cols=slice(0, N)):
+        def block_product(acc, m, c, cols):
             if m < EARLY:
                 block = weights[c][:, m * P : (m + 1) * P]
             else:
                 block = last_weights[:, c, (m - EARLY) * P : (m - EARLY + 1) * P]
-            nc.tensor.matmul(
-                acc[:, cols],
-                block,
-                scaled[c][:, cols],
-                start=(c == 0),
-                stop=(c == CB - 1),
-            )
+            nc.tensor.matmul(acc[:, cols], block, scaled[c][:, cols], start=(c == 0), stop=(c == CB - 1))
+
+        def add_next(m):
+            block_product(accs[m], m, added[m], slice(0, N))
+            added[m] += 1
+
+        def leave(acc, m, cols):
+            nc.vector.tensor_tensor(results[m][:, cols], acc[:, cols], rstd[:, cols], MULT)
+            nc.sync.dma_start(out[m * P : (m + 1) * P, cols], results[m][:, cols])
 
         picked = [held.tile([P, N], F32, name=f"picked{c}") for c in range(CB)]
         squares = [held.tile([P, N], F32, name=f"squares{c}") for c in range(CB)]
@@ -95,7 +97,7 @@ def tile_mla_kernel(tc, cache, gain, w_up, offs, out):
             nc.vector.tensor_copy(rounded[c][:], squares[c][:])
             nc.vector.tensor_tensor(left_over[c][:], squares[c][:], rounded[c][:], SUBTRACT)
             for m in range(EARLY):
-                add_product(accs[m], m, c)
+                add_next(m)
             for h in range(HALVES):
                 cols = slice(h * NH, (h + 1) * NH)
                 total = sums[h][:, cols]
@@ -105,13 +107,16 @@ def tile_mla_kernel(tc, cache, gain, w_up, offs, out):
         for c in range(CB - LATE, CB):
             if c == CB - 1:
                 for m in range(FILL):
-                    add_product(accs[m], m, c - 1)
+                    add_next(m)
             for q in range(Q):
                 cols = slice(q * NQ, (q + 1) * NQ)
                 piece = offsets[:, q * (NQ // 16) : (q + 1) * (NQ // 16)]
                 nc.scalar.activation(picked[c][:, cols], windows[c][:].indirect(piece), COPY)
+                nc.vector.tensor_scalar_mul(scaled[c][:, cols], picked[c][:, cols], gains[:, c : c + 1])
                 nc.vector.tensor_tensor(squares[c][:, cols], picked[c][:, cols], picked[c][:, cols], MULT)
                 h = cols.start // NH
+                if c == CB - 1 and q == Q - 1:
+                    add_next(0)
                 nc.tensor.matmul(
                     sums[h][:, cols],
                     ones[:],
@@ -119,27 +124,27 @@ def tile_mla_kernel(tc, cache, gain, w_up, offs, out):
                     start=False,
                     stop=(c == CB - 1 and cols.stop == (h + 1) * NH),
                 )
-            nc.vector.tensor_scalar_mul(scaled[c][:], picked[c][:], gains[:, c : c + 1])
 
         rstd = held.tile([P, N], F32, name="rstd")
         for h in range(HALVES):
             cols = slice(h * NH, (h + 1) * NH)
             nc.scalar.activation(rstd[:, cols], sums[h][:, cols], RSQRT, scale=1.0 / C)
-            accs.append(psum.tile([P, N], F32, name=f"acc{BANKED + h}", tag=f"sums{h}"))
+            accs.append(psum.tile([P, N], F32, name=f"acc{EARLY + h}", tag=f"sums{h}"))
 
-        for m in range(MB):
-            first = 0 if m >= EARLY else CB - 1 if m < FILL else CB - LATE
-            result = staged.tile([P, N], F32, name="result")
-            if m < MB - 1:
-                parts = [(accs[m], slice(0, N))]
-            else:
-                spare = psum.tile([P, N], F32, name="spare", tag="acc0")
-                parts = [(accs[m], slice(0, NH)), (spare, slice(NH, N))]
-            width = NH if m in (0, MB - 1) else N
-            for acc, part in parts:
-                for c in range(first, CB):
-                    add_product(acc, m, c, part)
-                for begin in range(part.start, part.stop, width):
-                    cols = slice(begin, begin + width)
-                    nc.vector.tensor_tensor(result[:, cols], acc[:, cols], rstd[:, cols], MULT)
-                    nc.sync.dma_start(out[m * P : (m + 1) * P, cols], result[:, cols])
+        for m in range(2):
+            for c in range(added[m], CB):
+                add_next(m)
+        for h in range(HALVES):
+            for m in range(2):
+                leave(accs[m], m, slice(h * NH, (h + 1) * NH))
+        for m in range(2, MB - 1):
+            for c in range(added[m], CB):
+                add_next(m)
+            leave(accs[m], m, slice(0, N))
+
+        spare = psum.tile([P, N], F32, name="spare", tag="acc0")
+        for h, acc in enumerate([accs[MB - 1], spare]):
+            cols = slice(h * NH, (h + 1) * NH)
+            for c in range(CB):
+                block_product(acc, MB - 1, c, cols)
+            leave(acc, MB - 1, cols)

@@ -63,7 +63,7 @@ def tile_mla_kernel(tc, cache, gain, w_up, offs, out):
 
         zeros = held.tile([P, N], BF16, name="zeros")
         nc.vector.memset(zeros[:], 0.0)
-        for w in range(3 * 4096 // 2 // N):
+        for w in range(2 * 4096 // N):
             nc.tensor.matmul(sums[0][:], ones_bf16[:], zeros[:], start=True, stop=True)
         accs = [psum.tile([P, N], F32, name=f"acc{m}") for m in range(EARLY)]
         scaled = [held.tile([P, N], BF16, name=f"scaled{c}") for c in range(CB)]

import concourse.mybir as mybir

F32 = mybir.dt.float32
BF16 = mybir.dt.bfloat16
U16 = mybir.dt.uint16
MULT = mybir.AluOpType.mult
SUBTRACT = mybir.AluOpType.subtract
COPY = mybir.ActivationFunctionType.Copy
SQUARE = mybir.ActivationFunctionType.Square
RSQRT = mybir.ActivationFunctionType.Abs_reciprocal_sqrt

P = 128
C, S, N, M = 512, 2048, 512, 1024
CB = C // P
MB = M // P
HALVES = 2
EARLY = MB - HALVES
LATE = 2
EARLY_M = EARLY * P
Q = 4
NQ = N // Q
NH = N // HALVES
FILL = 3

FLOPS = 2 * C * M * N


def tile_mla_kernel(tc, cache, gain, w_up, offs, out):
    nc = tc.nc
    with (
        tc.tile_pool(name="held", bufs=1) as held,
        tc.psum_pool(name="psum", bufs=1) as psum,
    ):
        cache_blocks = cache.rearrange("(p c) s -> p c s", p=P)
        w_up_blocks = w_up.rearrange("(p c) m -> p c m", p=P)

        offsets = held.tile([P, N // 16], U16, name="offsets")
        windows = [held.tile([P, S], F32, name=f"window{c}") for c in range(CB)]
        weights = [held.tile([P, EARLY_M], BF16, name=f"weights{c}") for c in range(CB)]
        last_weights = held.tile([P, CB, M - EARLY_M], BF16, name="last_weights")
        for c in range(CB):
            nc.sync.dma_start(windows[c][:], cache_blocks[:, c, :])
            if c == 0:
                nc.sync.dma_start(offsets[:], offs)
            if c < CB - LATE:
                nc.sync.dma_start(weights[c][:], w_up_blocks[:, c, :EARLY_M])
        for c in range(CB - LATE, CB):
            nc.sync.dma_start(weights[c][:], w_up_blocks[:, c, :EARLY_M])
        nc.sync.dma_start(last_weights[:], w_up_blocks[:, :, EARLY_M:])

        gains = held.tile([P, CB], F32, name="gains")
        nc.scalar.dma_start(gains[:], gain.rearrange("(p c) o -> p (c o)", p=P))

        ones = held.tile([P, P], F32, name="ones")
        nc.vector.memset(ones[:], 1.0)
        ones_bf16 = held.tile([P, P], BF16, name="ones_bf16")
        nc.vector.memset(ones_bf16[:], 1.0)

        warm = held.tile([P, 1], F32, name="warm")
        nc.scalar.activation(warm[:], ones[:, 0:1], RSQRT)

        sums = [psum.tile([P, N], F32, name=f"sums{h}") for h in range(HALVES)]

        zeros = held.tile([P, N], BF16, name="zeros")
        nc.vector.memset(zeros[:], 0.0)
        for w in range(2 * 4096 // N):
            nc.tensor.matmul(sums[0][:], ones_bf16[:], zeros[:], start=True, stop=True)
        accs = [psum.tile([P, N], F32, name=f"acc{m}") for m in range(EARLY)]
        scaled = [held.tile([P, N], BF16, name=f"scaled{c}") for c in range(CB)]
        results = [held.tile([P, N], F32, name=f"result{m}") for m in range(MB)]
        added = [0] * MB

        def block_product(acc, m, c, cols):
            if m < EARLY:
                block = weights[c][:, m * P : (m + 1) * P]
            else:
                block = last_weights[:, c, (m - EARLY) * P : (m - EARLY + 1) * P]
            nc.tensor.matmul(acc[:, cols], block, scaled[c][:, cols], start=(c == 0), stop=(c == CB - 1))

        def add_next(m):
            block_product(accs[m], m, added[m], slice(0, N))
            added[m] += 1

        def leave(acc, m, cols):
            nc.vector.tensor_tensor(results[m][:, cols], acc[:, cols], rstd[:, cols], MULT)
            nc.sync.dma_start(out[m * P : (m + 1) * P, cols], results[m][:, cols])

        picked = [held.tile([P, N], F32, name=f"picked{c}") for c in range(CB)]
        squares = [held.tile([P, N], F32, name=f"squares{c}") for c in range(CB)]

        rounded = [held.tile([P, N], BF16, name=f"rounded{c}") for c in range(CB - LATE)]
        left_over = [held.tile([P, N], BF16, name=f"left_over{c}") for c in range(CB - LATE)]
        for c in range(CB - LATE):
            nc.scalar.activation(picked[c][:], windows[c][:].indirect(offsets[:]), COPY)
            nc.vector.tensor_scalar_mul(scaled[c][:], picked[c][:], gains[:, c : c + 1])
            nc.scalar.activation(squares[c][:], picked[c][:], SQUARE)
            nc.vector.tensor_copy(rounded[c][:], squares[c][:])
            nc.vector.tensor_tensor(left_over[c][:], squares[c][:], rounded[c][:], SUBTRACT)
            for m in range(EARLY):
                add_next(m)
            for h in range(HALVES):
                cols = slice(h * NH, (h + 1) * NH)
                total = sums[h][:, cols]
                nc.tensor.matmul(total, ones_bf16[:], rounded[c][:, cols], start=(c == 0), stop=False)
                nc.tensor.matmul(total, ones_bf16[:], left_over[c][:, cols], start=False, stop=False)

        for c in range(CB - LATE, CB):
            if c == CB - 1:
                for m in range(FILL):
                    add_next(m)
            for q in range(Q):
                cols = slice(q * NQ, (q + 1) * NQ)
                piece = offsets[:, q * (NQ // 16) : (q + 1) * (NQ // 16)]
                nc.scalar.activation(picked[c][:, cols], windows[c][:].indirect(piece), COPY)
                nc.vector.tensor_scalar_mul(scaled[c][:, cols], picked[c][:, cols], gains[:, c : c + 1])
                nc.vector.tensor_tensor(squares[c][:, cols], picked[c][:, cols], picked[c][:, cols], MULT)
                h = cols.start // NH
                if c == CB - 1 and q == Q - 1:
                    add_next(0)
                nc.tensor.matmul(
                    sums[h][:, cols],
                    ones[:],
                    squares[c][:, cols],
                    start=False,
                    stop=(c == CB - 1 and cols.stop == (h + 1) * NH),
                )

        rstd = held.tile([P, N], F32, name="rstd")
        for h in range(HALVES):
            cols = slice(h * NH, (h + 1) * NH)
            nc.scalar.activation(rstd[:, cols], sums[h][:, cols], RSQRT, scale=1.0 / C)
            accs.append(psum.tile([P, N], F32, name=f"acc{EARLY + h}", tag=f"sums{h}"))

        for m in range(2):
            for c in range(added[m], CB):
                add_next(m)
        for h in range(HALVES):
            for m in range(2):
                leave(accs[m], m, slice(h * NH, (h + 1) * NH))
        for m in range(2, MB - 1):
            for c in range(added[m], CB):
                add_next(m)
            leave(accs[m], m, slice(0, N))

        spare = psum.tile([P, N], F32, name="spare", tag="acc0")
        for h, acc in enumerate([accs[MB - 1], spare]):
            cols = slice(h * NH, (h + 1) * NH)
            for c in range(CB):
                block_product(acc, MB - 1, c, cols)
            leave(acc, MB - 1, cols)
